import numpy as np
import ml_dtypes


def mxq(x, axis, fmt="e4m3"):
    dtype, down = {"e4m3": (ml_dtypes.float8_e4m3fn, 7), "e5m2": (ml_dtypes.float8_e5m2, 14)}[fmt]
    v = np.moveaxis(np.asarray(x, np.float32).astype(ml_dtypes.bfloat16).astype(np.float64), axis, -1)
    blocks = v.reshape(v.shape[:-1] + (-1, 32))
    amax = np.abs(blocks).max(-1, keepdims=True)
    byte = np.maximum(np.where(amax > 0, np.frexp(amax)[1] - 1 + 127, 0) - down, 1)
    scale = np.exp2(byte - 127.0)
    codes = (blocks / scale).astype(np.float32).astype(dtype).astype(np.float64)
    return np.moveaxis((codes * scale).reshape(v.shape), -1, axis)


WIDE = False


def mx_kscale(k):
    if not WIDE:
        return np.ones(k)
    levels = np.array([20, -20, 10, -10, 0])
    a = np.random.permutation(np.resize(levels, k // 512 * 4)).reshape(k // 512, 4)
    idx = np.arange(k)
    return np.exp2(a[idx // 512, idx % 128 // 32])


BF16 = ml_dtypes.bfloat16


def bf(x):
    return np.asarray(x, np.float32).astype(BF16)


def f64(x):
    return np.asarray(x).astype(np.float64)


B, L, F, A = 512, 12, 256, 512


def setup_inputs():
    u = mx_kscale(L * A).reshape(L, A)
    thresh = 1.0 / (A * L) ** 0.5
    inp = {"x": bf(np.random.standard_normal((B, L, F)))}
    for i in range(L):
        inp[f"W_{i}"] = bf(np.random.uniform(-thresh, thresh, (i + 1, F, A)) / u[i])
    g = np.random.standard_normal((B, L, A)) * np.exp2(np.random.randint(-12, 1, (B, 1, 1))) * 16.0 * u
    inp["grad_out"] = bf(g)
    return inp


def reference(x, W_0, W_1, W_2, W_3, W_4, W_5, W_6, W_7, W_8, W_9, W_10, W_11, grad_out):
    Ws = [W_0, W_1, W_2, W_3, W_4, W_5, W_6, W_7, W_8, W_9, W_10, W_11]
    gq = mxq(f64(grad_out).reshape(B, L * A), 1, "e5m2")
    Wq = [mxq(f64(Ws[i]).reshape((i + 1) * F, A), 1, "e4m3") for i in range(L)]
    gx = []
    for l in range(L):
        wl = np.concatenate([Wq[i][l * F : (l + 1) * F] for i in range(l, L)], axis=1)
        gx.append(gq[:, l * A :] @ wl.T)
    return np.stack(gx, axis=1)

@@ -1,0 +1,180 @@
+from contextlib import ExitStack
+
+import concourse.mybir as mybir
+from concourse.masks import make_identity
+
+BF16 = mybir.dt.bfloat16
+F32 = mybir.dt.float32
+I32 = mybir.dt.int32
+U32 = mybir.dt.uint32
+U8 = mybir.dt.uint8
+E4M3_X4 = mybir.dt.float8_e4m3fn_x4
+E5M2_X4 = mybir.dt.float8_e5m2_x4
+
+B, L, F, A = 512, 12, 256, 512
+P = 128
+PACK = 4
+SLAB_ROWS = 2 * P
+PANEL_ROWS = 2 * SLAB_ROWS
+PAIRS = L // 2
+B_TILES = B // P
+
+RAW_ROUNDS = 6
+
+LAYER_PAIRS = L * (L + 1) // 2
+FLOPS = 2 * B * F * A * LAYER_PAIRS
+BYTES = 2 * F * A * LAYER_PAIRS + 2 * B * L * A + 4 * B * L * F
+
+
+def load_slab(nc, raw_slab, rows):
+    nc.sync.dma_start(
+        out=raw_slab.rearrange("p (r a) -> p r a", r=2),
+        in_=rows.rearrange("(p r) a -> p r a", r=2),
+    )
+
+
+def turn_slab(nc, bank, raw_slab, identity):
+    words = raw_slab.bitcast(F32)
+    for c in range(4):
+        nc.tensor.transpose(bank[:, c, :], words[:, c * P : (c + 1) * P], identity)
+
+
+def regroup(copy, grouped_slab, bank):
+    copy(
+        out=grouped_slab.bitcast(F32).rearrange("q (p c) -> q p c", c=4),
+        in_=bank.rearrange("q c p -> q p c"),
+    )
+
+
+def tile_decoder_pa_kernel(
+    tc, x, W_0, W_1, W_2, W_3, W_4, W_5, W_6, W_7, W_8, W_9, W_10, W_11, grad_out, out
+):
+    nc = tc.nc
+    weights = [W_0, W_1, W_2, W_3, W_4, W_5, W_6, W_7, W_8, W_9, W_10, W_11]
+
+    rounds = []
+    for j in reversed(range(PAIRS)):
+        for m in reversed(range(j, PAIRS)):
+            rounds.append(("weights", j, m))
+            if m == PAIRS - 1:
+                rounds.append(("gradients", j, j))
+
+    def panel_slabs(kind, j, i):
+        if kind == "gradients":
+            return [grad_out[h * SLAB_ROWS : (h + 1) * SLAB_ROWS, i, :] for h in range(2)]
+        return [weights[i][l] for l in (2 * j, 2 * j + 1) if l <= i]
+
+    with ExitStack() as stack:
+        const = stack.enter_context(tc.tile_pool(name="const", bufs=1))
+        raw_pool = stack.enter_context(tc.tile_pool(name="raw", bufs=RAW_ROUNDS))
+        grouped_pool = stack.enter_context(tc.tile_pool(name="grouped", bufs=4))
+        weight_pool = stack.enter_context(tc.tile_pool(name="weight", bufs=6))
+        gradient_pool = stack.enter_context(tc.tile_pool(name="gradient", bufs=1))
+        result_pool = stack.enter_context(tc.tile_pool(name="result", bufs=4))
+        turn_pool = stack.enter_context(tc.psum_pool(name="turn", bufs=4))
+        sum_pool = stack.enter_context(tc.psum_pool(name="sum", bufs=1))
+
+        identity = const.tile([P, P], F32, name="identity")
+        make_identity(nc, identity[:])
+
+        stack.enter_context(tc.manual_schedule())
+
+        raw_tiles = {}
+        gradient_operands = {}
+        sums = {}
+
+        def fetch(n):
+            kind, j, m = rounds[n]
+            raw = raw_pool.tile([P, 4, 2 * A], BF16, name="raw")
+            for k in range(2):
+                for h, rows in enumerate(panel_slabs(kind, j, 2 * m + k)):
+                    load_slab(nc, raw[:, 2 * k + h, :], rows)
+            raw_tiles[n] = raw
+
+        def prepare(n):
+            kind, j, m = rounds[n]
+            raw = raw_tiles[n]
+            slab_counts = [len(panel_slabs(kind, j, 2 * m + k)) for k in range(2)]
+
+            banks = {}
+            for k in range(2):
+                for h in range(slab_counts[k]):
+                    bank = turn_pool.tile([P, 4, P], F32, name="bank")
+                    turn_slab(nc, bank, raw[:, 2 * k + h, :], identity[:])
+                    banks[(k, h)] = bank
+
+            grouped_tiles = []
+            for k in range(2):
+                grouped = grouped_pool.tile([P, PANEL_ROWS * PACK], BF16, name="grouped", align_bytes=64)
+                for h in range(slab_counts[k]):
+                    copy = nc.scalar.copy if h == 0 else nc.vector.tensor_copy
+                    columns = slice(h * SLAB_ROWS * PACK, (h + 1) * SLAB_ROWS * PACK)
+                    regroup(copy, grouped[:, columns], banks[(k, h)])
+                grouped_tiles.append(grouped)
+
+            operands = []
+            for k in range(2):
+                i = 2 * m + k
+                if kind == "gradients":
+                    codes = gradient_pool.tile([P, PANEL_ROWS], U32, name="g_codes%d" % i, align_bytes=64)
+                    scales = gradient_pool.tile([P, PANEL_ROWS], U8, name="g_scales%d" % i, align_bytes=64)
+                    packed = E5M2_X4
+                else:
+                    codes = weight_pool.tile([P, PANEL_ROWS], U32, name="w_codes", align_bytes=64)
+                    scales = weight_pool.tile([P, PANEL_ROWS], U8, name="w_scales", align_bytes=64)
+                    packed = E4M3_X4
+                rows = slab_counts[k] * SLAB_ROWS
+                if rows < PANEL_ROWS:
+                    nc.vector.memset(codes[:, rows:].bitcast(I32), 0)
+                    nc.vector.memset(scales[:, rows:].bitcast(I32), 0)
+                nc.vector.quantize_mx(
+                    out=codes[:, :rows].bitcast(packed),
+                    scales=scales[:, :rows],
+                    in_=grouped_tiles[k][:, : rows * PACK],
+                )
+                operands.append((codes, scales))
+                if kind == "gradients":
+                    gradient_operands[i] = (codes, scales)
+
+            if n + RAW_ROUNDS < len(rounds):
+                fetch(n + RAW_ROUNDS)
+            return operands
+
+        def multiply(j, m, weight_operands):
+            first, last = m == PAIRS - 1, m == j
+            for t in range(B_TILES):
+                if first:
+                    sums[t] = sum_pool.tile([P, PANEL_ROWS], F32, name="sum%d" % t)
+                b_columns = slice(t * P, (t + 1) * P)
+                for k in range(2):
+                    g_codes, g_scales = gradient_operands[2 * m + k]
+                    w_codes, w_scales = weight_operands[k]
+                    nc.tensor.matmul_mx(
+                        out=sums[t][:],
+                        lhsT=g_codes[:, b_columns].bitcast(E5M2_X4),
+                        lhsT_scale=g_scales[:, b_columns],
+                        rhs=w_codes[:].bitcast(E4M3_X4),
+                        rhs_scale=w_scales[:],
+                        start=(first and k == 0),
+                        stop=(last and k == 1),
+                    )
+            if last:
+                for t in range(B_TILES):
+                    result = result_pool.tile([P, PANEL_ROWS], F32, name="result")
+                    nc.scalar.copy(out=result[:], in_=sums[t][:])
+                    nc.scalar.dma_start(
+                        out=out[t * P : (t + 1) * P, 2 * j : 2 * j + 2, :].rearrange("b l f -> b (l f)"),
+                        in_=result[:],
+                    )
+
+        for n in range(RAW_ROUNDS):
+            fetch(n)
+
+        waiting = None
+        for n, (kind, j, m) in enumerate(rounds):
+            operands = prepare(n)
+            if kind == "weights":
+                if waiting is not None:
+                    multiply(*waiting)
+                waiting = (j, m, operands)
+        multiply(*waiting)

@@ -26,17 +26,10 @@ FLOPS = 2 * B * F * A * LAYER_PAIRS
 BYTES = 2 * F * A * LAYER_PAIRS + 2 * B * L * A + 4 * B * L * F
 
 
-def load_slab(nc, raw_slab, rows):
-    nc.sync.dma_start(
-        out=raw_slab.rearrange("p (r a) -> p r a", r=2),
-        in_=rows.rearrange("(p r) a -> p r a", r=2),
-    )
-
-
-def turn_slab(nc, bank, raw_slab, identity):
-    words = raw_slab.bitcast(F32)
-    for c in range(4):
-        nc.tensor.transpose(bank[:, c, :], words[:, c * P : (c + 1) * P], identity)
+def turn_slab(nc, bank, words, identity):
+    for r in range(2):
+        for u in range(2):
+            nc.tensor.transpose(bank[:, 2 * r + u, :], words[:, r, u * P : (u + 1) * P], identity)
 
 
 def regroup(copy, grouped_slab, bank):
@@ -59,10 +52,8 @@ def tile_decoder_pa_kernel(
             if m == PAIRS - 1:
                 rounds.append(("gradients", j, j))
 
-    def panel_slabs(kind, j, i):
-        if kind == "gradients":
-            return [grad_out[h * SLAB_ROWS : (h + 1) * SLAB_ROWS, i, :] for h in range(2)]
-        return [weights[i][l] for l in (2 * j, 2 * j + 1) if l <= i]
+    def slabs_in_panel(kind, j, i):
+        return 1 if kind == "weights" and i == 2 * j else 2
 
     with ExitStack() as stack:
         const = stack.enter_context(tc.tile_pool(name="const", bufs=1))
@@ -79,28 +70,45 @@ def tile_decoder_pa_kernel(
 
         stack.enter_context(tc.manual_schedule())
 
-        raw_tiles = {}
+        raw_slabs = {}
         gradient_operands = {}
         sums = {}
 
         def fetch(n):
             kind, j, m = rounds[n]
             raw = raw_pool.tile([P, 4, 2 * A], BF16, name="raw")
-            for k in range(2):
-                for h, rows in enumerate(panel_slabs(kind, j, 2 * m + k)):
-                    load_slab(nc, raw[:, 2 * k + h, :], rows)
-            raw_tiles[n] = raw
+            words = raw[:].bitcast(F32)
+            views = {}
+            for c in range(2):
+                if kind == "weights":
+                    i = 2 * m + c
+                    count = slabs_in_panel(kind, j, i)
+                    nc.sync.dma_start(
+                        out=raw[:, 2 * c : 2 * c + count, :],
+                        in_=weights[i][2 * j : 2 * j + count].rearrange("l (p r) a -> p l (r a)", r=2),
+                    )
+                    for h in range(count):
+                        views[(c, h)] = words[:, 2 * c + h, :].rearrange("p (r w) -> p r w", r=2)
+                else:
+                    nc.sync.dma_start(
+                        out=raw[:, 2 * c : 2 * c + 2, :],
+                        in_=grad_out[c * SLAB_ROWS : (c + 1) * SLAB_ROWS, 2 * m : 2 * m + 2, :].rearrange(
+                            "(p r) i a -> p r (i a)", r=2
+                        ),
+                    )
+                    for k in range(2):
+                        views[(k, c)] = words[:, 2 * c : 2 * c + 2, k * A // 2 : (k + 1) * A // 2]
+            raw_slabs[n] = views
 
         def prepare(n):
             kind, j, m = rounds[n]
-            raw = raw_tiles[n]
-            slab_counts = [len(panel_slabs(kind, j, 2 * m + k)) for k in range(2)]
+            slab_counts = [slabs_in_panel(kind, j, 2 * m + k) for k in range(2)]
 
             banks = {}
             for k in range(2):
                 for h in range(slab_counts[k]):
                     bank = turn_pool.tile([P, 4, P], F32, name="bank")
-                    turn_slab(nc, bank, raw[:, 2 * k + h, :], identity[:])
+                    turn_slab(nc, bank, raw_slabs[n][(k, h)], identity[:])
                     banks[(k, h)] = bank
 
             grouped_tiles = []
@@ -162,7 +170,7 @@ def tile_decoder_pa_kernel(
                 for t in range(B_TILES):
                     result = result_pool.tile([P, PANEL_ROWS], F32, name="result")
                     nc.scalar.copy(out=result[:], in_=sums[t][:])
-                    nc.scalar.dma_start(
+                    nc.sync.dma_start(
                         out=out[t * P : (t + 1) * P, 2 * j : 2 * j + 2, :].rearrange("b l f -> b (l f)"),
                         in_=result[:],
                     )

@@ -61,7 +61,7 @@ def tile_decoder_pa_kernel(
         grouped_pool = stack.enter_context(tc.tile_pool(name="grouped", bufs=4))
         weight_pool = stack.enter_context(tc.tile_pool(name="weight", bufs=6))
         gradient_pool = stack.enter_context(tc.tile_pool(name="gradient", bufs=1))
-        result_pool = stack.enter_context(tc.tile_pool(name="result", bufs=4))
+        result_pool = stack.enter_context(tc.tile_pool(name="result", bufs=2 * B_TILES))
         turn_pool = stack.enter_context(tc.psum_pool(name="turn", bufs=4))
         sum_pool = stack.enter_context(tc.psum_pool(name="sum", bufs=1))
 

@@ -68,8 +68,6 @@ def tile_decoder_pa_kernel(
         identity = const.tile([P, P], F32, name="identity")
         make_identity(nc, identity[:])
 
-        stack.enter_context(tc.manual_schedule())
-
         raw_slabs = {}
         gradient_operands = {}
         sums = {}

from contextlib import ExitStack

import concourse.mybir as mybir
from concourse.masks import make_identity

BF16 = mybir.dt.bfloat16
F32 = mybir.dt.float32
I32 = mybir.dt.int32
U32 = mybir.dt.uint32
U8 = mybir.dt.uint8
E4M3_X4 = mybir.dt.float8_e4m3fn_x4
E5M2_X4 = mybir.dt.float8_e5m2_x4

B, L, F, A = 512, 12, 256, 512
P = 128
PACK = 4
SLAB_ROWS = 2 * P
PANEL_ROWS = 2 * SLAB_ROWS
PAIRS = L // 2
B_TILES = B // P

RAW_ROUNDS = 6

LAYER_PAIRS = L * (L + 1) // 2
FLOPS = 2 * B * F * A * LAYER_PAIRS
BYTES = 2 * F * A * LAYER_PAIRS + 2 * B * L * A + 4 * B * L * F


def turn_slab(nc, bank, words, identity):
    for r in range(2):
        for u in range(2):
            nc.tensor.transpose(bank[:, 2 * r + u, :], words[:, r, u * P : (u + 1) * P], identity)


def regroup(copy, grouped_slab, bank):
    copy(
        out=grouped_slab.bitcast(F32).rearrange("q (p c) -> q p c", c=4),
        in_=bank.rearrange("q c p -> q p c"),
    )


def tile_decoder_pa_kernel(
    tc, x, W_0, W_1, W_2, W_3, W_4, W_5, W_6, W_7, W_8, W_9, W_10, W_11, grad_out, out
):
    nc = tc.nc
    weights = [W_0, W_1, W_2, W_3, W_4, W_5, W_6, W_7, W_8, W_9, W_10, W_11]

    rounds = []
    for j in reversed(range(PAIRS)):
        for m in reversed(range(j, PAIRS)):
            rounds.append(("weights", j, m))
            if m == PAIRS - 1:
                rounds.append(("gradients", j, j))

    def slabs_in_panel(kind, j, i):
        return 1 if kind == "weights" and i == 2 * j else 2

    with ExitStack() as stack:
        const = stack.enter_context(tc.tile_pool(name="const", bufs=1))
        raw_pool = stack.enter_context(tc.tile_pool(name="raw", bufs=RAW_ROUNDS))
        grouped_pool = stack.enter_context(tc.tile_pool(name="grouped", bufs=4))
        weight_pool = stack.enter_context(tc.tile_pool(name="weight", bufs=6))
        gradient_pool = stack.enter_context(tc.tile_pool(name="gradient", bufs=1))
        result_pool = stack.enter_context(tc.tile_pool(name="result", bufs=2 * B_TILES))
        turn_pool = stack.enter_context(tc.psum_pool(name="turn", bufs=4))
        sum_pool = stack.enter_context(tc.psum_pool(name="sum", bufs=1))

        identity = const.tile([P, P], F32, name="identity")
        make_identity(nc, identity[:])

        raw_slabs = {}
        gradient_operands = {}
        sums = {}

        def fetch(n):
            kind, j, m = rounds[n]
            raw = raw_pool.tile([P, 4, 2 * A], BF16, name="raw")
            words = raw[:].bitcast(F32)
            views = {}
            for c in range(2):
                if kind == "weights":
                    i = 2 * m + c
                    count = slabs_in_panel(kind, j, i)
                    nc.sync.dma_start(
                        out=raw[:, 2 * c : 2 * c + count, :],
                        in_=weights[i][2 * j : 2 * j + count].rearrange("l (p r) a -> p l (r a)", r=2),
                    )
                    for h in range(count):
                        views[(c, h)] = words[:, 2 * c + h, :].rearrange("p (r w) -> p r w", r=2)
                else:
                    nc.sync.dma_start(
                        out=raw[:, 2 * c : 2 * c + 2, :],
                        in_=grad_out[c * SLAB_ROWS : (c + 1) * SLAB_ROWS, 2 * m : 2 * m + 2, :].rearrange(
                            "(p r) i a -> p r (i a)", r=2
                        ),
                    )
                    for k in range(2):
                        views[(k, c)] = words[:, 2 * c : 2 * c + 2, k * A // 2 : (k + 1) * A // 2]
            raw_slabs[n] = views

        def prepare(n):
            kind, j, m = rounds[n]
            slab_counts = [slabs_in_panel(kind, j, 2 * m + k) for k in range(2)]

            banks = {}
            for k in range(2):
                for h in range(slab_counts[k]):
                    bank = turn_pool.tile([P, 4, P], F32, name="bank")
                    turn_slab(nc, bank, raw_slabs[n][(k, h)], identity[:])
                    banks[(k, h)] = bank

            grouped_tiles = []
            for k in range(2):
                grouped = grouped_pool.tile([P, PANEL_ROWS * PACK], BF16, name="grouped", align_bytes=64)
                for h in range(slab_counts[k]):
                    copy = nc.scalar.copy if h == 0 else nc.vector.tensor_copy
                    columns = slice(h * SLAB_ROWS * PACK, (h + 1) * SLAB_ROWS * PACK)
                    regroup(copy, grouped[:, columns], banks[(k, h)])
                grouped_tiles.append(grouped)

            operands = []
            for k in range(2):
                i = 2 * m + k
                if kind == "gradients":
                    codes = gradient_pool.tile([P, PANEL_ROWS], U32, name="g_codes%d" % i, align_bytes=64)
                    scales = gradient_pool.tile([P, PANEL_ROWS], U8, name="g_scales%d" % i, align_bytes=64)
                    packed = E5M2_X4
                else:
                    codes = weight_pool.tile([P, PANEL_ROWS], U32, name="w_codes", align_bytes=64)
                    scales = weight_pool.tile([P, PANEL_ROWS], U8, name="w_scales", align_bytes=64)
                    packed = E4M3_X4
                rows = slab_counts[k] * SLAB_ROWS
                if rows < PANEL_ROWS:
                    nc.vector.memset(codes[:, rows:].bitcast(I32), 0)
                    nc.vector.memset(scales[:, rows:].bitcast(I32), 0)
                nc.vector.quantize_mx(
                    out=codes[:, :rows].bitcast(packed),
                    scales=scales[:, :rows],
                    in_=grouped_tiles[k][:, : rows * PACK],
                )
                operands.append((codes, scales))
                if kind == "gradients":
                    gradient_operands[i] = (codes, scales)

            if n + RAW_ROUNDS < len(rounds):
                fetch(n + RAW_ROUNDS)
            return operands

        def multiply(j, m, weight_operands):
            first, last = m == PAIRS - 1, m == j
            for t in range(B_TILES):
                if first:
                    sums[t] = sum_pool.tile([P, PANEL_ROWS], F32, name="sum%d" % t)
                b_columns = slice(t * P, (t + 1) * P)
                for k in range(2):
                    g_codes, g_scales = gradient_operands[2 * m + k]
                    w_codes, w_scales = weight_operands[k]
                    nc.tensor.matmul_mx(
                        out=sums[t][:],
                        lhsT=g_codes[:, b_columns].bitcast(E5M2_X4),
                        lhsT_scale=g_scales[:, b_columns],
                        rhs=w_codes[:].bitcast(E4M3_X4),
                        rhs_scale=w_scales[:],
                        start=(first and k == 0),
                        stop=(last and k == 1),
                    )
            if last:
                for t in range(B_TILES):
                    result = result_pool.tile([P, PANEL_ROWS], F32, name="result")
                    nc.scalar.copy(out=result[:], in_=sums[t][:])
                    nc.sync.dma_start(
                        out=out[t * P : (t + 1) * P, 2 * j : 2 * j + 2, :].rearrange("b l f -> b (l f)"),
                        in_=result[:],
                    )

        for n in range(RAW_ROUNDS):
            fetch(n)

        waiting = None
        for n, (kind, j, m) in enumerate(rounds):
            operands = prepare(n)
            if kind == "weights":
                if waiting is not None:
                    multiply(*waiting)
                waiting = (j, m, operands)
        multiply(*waiting)
